import numpy as np
import ml_dtypes


def mxq(x, axis, fmt="e4m3"):
    dtype, down = {"e4m3": (ml_dtypes.float8_e4m3fn, 7), "e5m2": (ml_dtypes.float8_e5m2, 14)}[fmt]
    v = np.moveaxis(np.asarray(x, np.float32).astype(ml_dtypes.bfloat16).astype(np.float64), axis, -1)
    blocks = v.reshape(v.shape[:-1] + (-1, 32))
    amax = np.abs(blocks).max(-1, keepdims=True)
    byte = np.maximum(np.where(amax > 0, np.frexp(amax)[1] - 1 + 127, 0) - down, 1)
    scale = np.exp2(byte - 127.0)
    codes = (blocks / scale).astype(np.float32).astype(dtype).astype(np.float64)
    return np.moveaxis((codes * scale).reshape(v.shape), -1, axis)


WIDE = False


def mx_kscale(k):
    if not WIDE:
        return np.ones(k)
    levels = np.array([20, -20, 10, -10, 0])
    a = np.random.permutation(np.resize(levels, k // 512 * 4)).reshape(k // 512, 4)
    idx = np.arange(k)
    return np.exp2(a[idx // 512, idx % 128 // 32])


BF16 = ml_dtypes.bfloat16


def bf(x):
    return np.asarray(x, np.float32).astype(BF16)


def f64(x):
    return np.asarray(x).astype(np.float64)


B, C, O, E = 1024, 512, 512, 2
KERNEL = 3
PADDING = 1


def setup_inputs():
    u = mx_kscale(O)
    x = np.random.standard_normal((B, C, E, E))
    weights = np.random.random((E, E, O, C, KERNEL, KERNEL)) * 1.7 / np.sqrt(KERNEL * KERNEL * C) / u[None, None, :, None, None, None]
    g = np.random.standard_normal((B, O, E, E)) * np.exp2(np.random.randint(-12, 1, (B, 1, E, E))) * 16.0 * u[None, :, None, None]
    return {"x": bf(x), "weights": bf(weights), "grad_out": bf(g)}


def reference(x, weights, grad_out):
    gq = mxq(f64(grad_out), 1, "e5m2")
    wt = f64(weights)
    gx = np.zeros((B, C, E, E))
    for i in range(KERNEL):
        for j in range(KERNEL):
            w0, w1 = max(0, PADDING - i), min(E, E + PADDING - i)
            h0, h1 = max(0, PADDING - j), min(E, E + PADDING - j)
            wq = mxq(wt[h0:h1, w0:w1, :, :, i, j], 2, "e4m3")
            gs = gq[:, :, h0:h1, w0:w1].transpose(2, 3, 0, 1)
            prod = gs @ wq
            gx[:, :, w0 + i - PADDING:w1 + i - PADDING, h0 + j - PADDING:h1 + j - PADDING] += prod.transpose(2, 3, 1, 0)
    return gx

@@ -1,0 +1,115 @@
+from contextlib import ExitStack
+
+import concourse.mybir as mybir
+from concourse.masks import make_identity
+
+F32 = mybir.dt.float32
+BF16 = mybir.dt.bfloat16
+U32 = mybir.dt.uint32
+U8 = mybir.dt.uint8
+E4X4 = mybir.dt.float8_e4m3fn_x4
+E5X4 = mybir.dt.float8_e5m2_x4
+
+P = 128
+B, C, O = 1024, 512, 512
+S = B // P
+HW = 4
+T = 4
+CT = 4
+CW = C // CT
+N = CW * 4
+TAPS = 9
+
+FLOPS = 2 * B * (C * 4) * (O * HW)
+BYTES = 2 * (HW * O * C * 4) + 2 * (B * O * HW) + 4 * (B * C * 4)
+
+
+def tile_locallyconnected2d_t_kernel(tc, x, weights, grad_out, out):
+    nc = tc.nc
+    g_view = grad_out.rearrange("(p s) o h w -> p s (o h w)", s=S)
+    w_view = weights.rearrange("h w (t p) c i j -> (h w) p t (c i j)", p=P)
+    out_view = out.rearrange("(p s) c r q -> p s (c r q)", s=S)
+
+    with ExitStack() as ctx:
+        keep = ctx.enter_context(tc.tile_pool(name="keep", bufs=1))
+        graw_pool = ctx.enter_context(tc.tile_pool(name="graw", bufs=4))
+        ggrp_pool = ctx.enter_context(tc.tile_pool(name="ggrp", bufs=2))
+        wraw_pool = ctx.enter_context(tc.tile_pool(name="wraw", bufs=8))
+        wgrp_pool = ctx.enter_context(tc.tile_pool(name="wgrp", bufs=3))
+        osb_pool = ctx.enter_context(tc.tile_pool(name="osb", bufs=2))
+        psum = ctx.enter_context(tc.psum_pool(name="psum", bufs=8))
+
+        ident = keep.tile([P, P], F32)
+        make_identity(nc, ident[:])
+
+        g_codes = keep.tile([P, S, HW * P], U32, align_bytes=64)
+        g_scales = keep.tile([P, S, HW * P], U8, align_bytes=64)
+        w_codes = keep.tile([P, CT * HW, N], U32, align_bytes=64)
+        w_scales = keep.tile([P, CT * HW, N], U8, align_bytes=64)
+
+        g_raw = []
+        for pair in range(S // 2):
+            graw = graw_pool.tile([P, 2, O * HW], BF16)
+            nc.sync.dma_start(out=graw[:], in_=g_view[:, 2 * pair : 2 * pair + 2, :])
+            g_raw.append(graw)
+
+        for s in range(S):
+            words = g_raw[s // 2][:, s % 2, :].bitcast(F32).rearrange(
+                "p (t o h) -> p t h o", t=T, o=P, h=2
+            )
+            ggrp = ggrp_pool.tile([P, HW, P, T], BF16, align_bytes=64)
+            for h in range(2):
+                xt = psum.tile([P, T * P], F32, tag="bank")
+                for t in range(T):
+                    nc.tensor.transpose(xt[:, t * P : (t + 1) * P], words[:, t, h, :], ident[:])
+                src = xt[:].bitcast(BF16).rearrange("p (t b w) -> p w b t", t=T, b=P, w=2)
+                if h == 0:
+                    nc.vector.tensor_copy(out=ggrp[:, 0:2, :, :], in_=src)
+                else:
+                    nc.scalar.copy(out=ggrp[:, 2:4, :, :], in_=src)
+            nc.vector.quantize_mx(
+                out=g_codes[:, s, :].bitcast(E5X4),
+                scales=g_scales[:, s, :],
+                in_=ggrp[:].rearrange("p a b t -> p (a b t)"),
+            )
+
+        for ct in range(CT):
+            accs = []
+            for s in range(S):
+                acc = psum.tile([P, N], F32, tag="bank", name="acc%d" % s)
+                accs.append(acc)
+            osb = osb_pool.tile([P, S, N], F32)
+            for hw in range(HW):
+                h, w = hw // 2, hw % 2
+                wraw = wraw_pool.tile([P, T, CW * TAPS], BF16)
+                nc.sync.dma_start(
+                    out=wraw[:], in_=w_view[hw][:, :, ct * CW * TAPS : (ct + 1) * CW * TAPS]
+                )
+                wgrp = wgrp_pool.tile([P, N * T], BF16, align_bytes=64)
+                src = wraw[:].rearrange("p t (c i j) -> p c t i j", i=3, j=3)
+                dst = wgrp[:].rearrange("p (c i j t) -> p c t i j", i=2, j=2, t=T)
+                for r in range(2):
+                    nc.vector.tensor_copy(
+                        out=dst[:, :, :, r, :], in_=src[:, :, :, 1 - w + r, 1 - h : 3 - h]
+                    )
+                k = ct * HW + hw
+                nc.vector.quantize_mx(
+                    out=w_codes[:, k, :].bitcast(E4X4), scales=w_scales[:, k, :], in_=wgrp[:]
+                )
+                for s in range(S):
+                    nc.tensor.matmul_mx(
+                        out=accs[s][:],
+                        lhsT=g_codes[:, s, hw * P : (hw + 1) * P].bitcast(E5X4),
+                        lhsT_scale=g_scales[:, s, hw * P : (hw + 1) * P],
+                        rhs=w_codes[:, k, :].bitcast(E4X4),
+                        rhs_scale=w_scales[:, k, :],
+                        start=(hw == 0),
+                        stop=(hw == HW - 1),
+                    )
+            for s in range(S):
+                nc.scalar.copy(out=osb[:, s, :], in_=accs[s][:])
+                if s % 4 == 3:
+                    nc.scalar.dma_start(
+                        out=out_view[:, s - 3 : s + 1, ct * N : (ct + 1) * N],
+                        in_=osb[:, s - 3 : s + 1, :],
+                    )

@@ -19,6 +19,9 @@ CT = 4
 CW = C // CT
 N = CW * 4
 TAPS = 9
+CH = 2
+SH = 4
+WBUFS = 4
 
 FLOPS = 2 * B * (C * 4) * (O * HW)
 BYTES = 2 * (HW * O * C * 4) + 2 * (B * O * HW) + 4 * (B * C * 4)
@@ -29,15 +32,15 @@ def tile_locallyconnected2d_t_kernel(tc, x, weights, grad_out, out):
     g_view = grad_out.rearrange("(p s) o h w -> p s (o h w)", s=S)
     w_view = weights.rearrange("h w (t p) c i j -> (h w) p t (c i j)", p=P)
     out_view = out.rearrange("(p s) c r q -> p s (c r q)", s=S)
+    chunks = [(half, hw) for half in range(CT // CH) for hw in range(HW)]
 
     with ExitStack() as ctx:
         keep = ctx.enter_context(tc.tile_pool(name="keep", bufs=1))
-        graw_pool = ctx.enter_context(tc.tile_pool(name="graw", bufs=4))
-        ggrp_pool = ctx.enter_context(tc.tile_pool(name="ggrp", bufs=2))
-        wraw_pool = ctx.enter_context(tc.tile_pool(name="wraw", bufs=8))
-        wgrp_pool = ctx.enter_context(tc.tile_pool(name="wgrp", bufs=3))
-        osb_pool = ctx.enter_context(tc.tile_pool(name="osb", bufs=2))
-        psum = ctx.enter_context(tc.psum_pool(name="psum", bufs=8))
+        big = ctx.enter_context(tc.tile_pool(name="big", bufs=4))
+        grp = ctx.enter_context(tc.tile_pool(name="grp", bufs=4))
+        wraw_pool = ctx.enter_context(tc.tile_pool(name="wraw", bufs=WBUFS))
+        psum = ctx.enter_context(tc.psum_pool(name="psum", bufs=1))
+        ctx.enter_context(tc.manual_schedule())
 
         ident = keep.tile([P, P], F32)
         make_identity(nc, ident[:])
@@ -48,68 +51,118 @@ def tile_locallyconnected2d_t_kernel(tc, x, weights, grad_out, out):
         w_scales = keep.tile([P, CT * HW, N], U8, align_bytes=64)
 
         g_raw = []
-        for pair in range(S // 2):
-            graw = graw_pool.tile([P, 2, O * HW], BF16)
-            nc.sync.dma_start(out=graw[:], in_=g_view[:, 2 * pair : 2 * pair + 2, :])
+        for quad in range(S // 4):
+            graw = big.tile([P, 4, O * HW], BF16, tag="big", name="graw")
+            for pair in range(2):
+                nc.sync.dma_start(
+                    out=graw[:, 2 * pair : 2 * pair + 2, :],
+                    in_=g_view[:, 4 * quad + 2 * pair : 4 * quad + 2 * pair + 2, :],
+                )
             g_raw.append(graw)
 
+        w_raw = {}
+
+        def load_chunk(k):
+            half, hw = chunks[k]
+            wraw = wraw_pool.tile([P, T, CH * CW * TAPS], BF16, name="wraw")
+            width = CH * CW * TAPS
+            nc.sync.dma_start(out=wraw[:], in_=w_view[hw][:, :, half * width : (half + 1) * width])
+            w_raw[k] = wraw
+
+        for k in range(WBUFS):
+            load_chunk(k)
+
+        def quantise_g(s, ggrp):
+            nc.vector.quantize_mx(
+                out=g_codes[:, s, :].bitcast(E5X4), scales=g_scales[:, s, :], in_=ggrp[:]
+            )
+
+        waiting = None
         for s in range(S):
-            words = g_raw[s // 2][:, s % 2, :].bitcast(F32).rearrange(
+            words = g_raw[s // 4][:, s % 4, :].bitcast(F32).rearrange(
                 "p (t o h) -> p t h o", t=T, o=P, h=2
             )
-            ggrp = ggrp_pool.tile([P, HW, P, T], BF16, align_bytes=64)
+            ggrp = grp.tile([P, HW * P * T], BF16, align_bytes=64, tag="grp", name="ggrp")
+            dst = ggrp[:].rearrange("p (a b t) -> p a b t", a=HW, b=P, t=T)
             for h in range(2):
-                xt = psum.tile([P, T * P], F32, tag="bank")
+                xt = psum.tile([P, T * P], F32, tag="bank%d" % ((2 * s + h) % 8), name="xt")
                 for t in range(T):
                     nc.tensor.transpose(xt[:, t * P : (t + 1) * P], words[:, t, h, :], ident[:])
                 src = xt[:].bitcast(BF16).rearrange("p (t b w) -> p w b t", t=T, b=P, w=2)
                 if h == 0:
-                    nc.vector.tensor_copy(out=ggrp[:, 0:2, :, :], in_=src)
+                    nc.vector.tensor_copy(out=dst[:, 0:2, :, :], in_=src)
                 else:
-                    nc.scalar.copy(out=ggrp[:, 2:4, :, :], in_=src)
-            nc.vector.quantize_mx(
-                out=g_codes[:, s, :].bitcast(E5X4),
-                scales=g_scales[:, s, :],
-                in_=ggrp[:].rearrange("p a b t -> p (a b t)"),
-            )
+                    nc.scalar.copy(out=dst[:, 2:4, :, :], in_=src)
+            if waiting is not None:
+                quantise_g(s - 1, waiting)
+            waiting = ggrp
+        quantise_g(S - 1, waiting)
 
-        for ct in range(CT):
-            accs = []
-            for s in range(S):
-                acc = psum.tile([P, N], F32, tag="bank", name="acc%d" % s)
-                accs.append(acc)
-            osb = osb_pool.tile([P, S, N], F32)
-            for hw in range(HW):
-                h, w = hw // 2, hw % 2
-                wraw = wraw_pool.tile([P, T, CW * TAPS], BF16)
-                nc.sync.dma_start(
-                    out=wraw[:], in_=w_view[hw][:, :, ct * CW * TAPS : (ct + 1) * CW * TAPS]
-                )
-                wgrp = wgrp_pool.tile([P, N * T], BF16, align_bytes=64)
-                src = wraw[:].rearrange("p t (c i j) -> p c t i j", i=3, j=3)
+        def prepare_chunk(k):
+            half, hw = chunks[k]
+            h, w = hw // 2, hw % 2
+            src = w_raw[k][:].rearrange("p t (c i j) -> p c t i j", i=3, j=3)
+            tiles = []
+            for a in range(CH):
+                wgrp = grp.tile([P, N * T], BF16, align_bytes=64, tag="grp", name="wgrp")
                 dst = wgrp[:].rearrange("p (c i j t) -> p c t i j", i=2, j=2, t=T)
                 for r in range(2):
                     nc.vector.tensor_copy(
-                        out=dst[:, :, :, r, :], in_=src[:, :, :, 1 - w + r, 1 - h : 3 - h]
+                        out=dst[:, :, :, r, :],
+                        in_=src[:, a * CW : (a + 1) * CW, :, 1 - w + r, 1 - h : 3 - h],
                     )
-                k = ct * HW + hw
+                tiles.append(wgrp)
+            for a in range(CH):
+                idx = (half * CH + a) * HW + hw
                 nc.vector.quantize_mx(
-                    out=w_codes[:, k, :].bitcast(E4X4), scales=w_scales[:, k, :], in_=wgrp[:]
+                    out=w_codes[:, idx, :].bitcast(E4X4), scales=w_scales[:, idx, :], in_=tiles[a][:]
                 )
-                for s in range(S):
-                    nc.tensor.matmul_mx(
-                        out=accs[s][:],
-                        lhsT=g_codes[:, s, hw * P : (hw + 1) * P].bitcast(E5X4),
-                        lhsT_scale=g_scales[:, s, hw * P : (hw + 1) * P],
-                        rhs=w_codes[:, k, :].bitcast(E4X4),
-                        rhs_scale=w_scales[:, k, :],
-                        start=(hw == 0),
-                        stop=(hw == HW - 1),
-                    )
-            for s in range(S):
-                nc.scalar.copy(out=osb[:, s, :], in_=accs[s][:])
-                if s % 4 == 3:
-                    nc.scalar.dma_start(
-                        out=out_view[:, s - 3 : s + 1, ct * N : (ct + 1) * N],
-                        in_=osb[:, s - 3 : s + 1, :],
-                    )
+
+        def mx_pass(acc, s, ct, hw):
+            idx = ct * HW + hw
+            nc.tensor.matmul_mx(
+                out=acc[:],
+                lhsT=g_codes[:, s, hw * P : (hw + 1) * P].bitcast(E5X4),
+                lhsT_scale=g_scales[:, s, hw * P : (hw + 1) * P],
+                rhs=w_codes[:, idx, :].bitcast(E4X4),
+                rhs_scale=w_scales[:, idx, :],
+                start=(hw == 0),
+                stop=(hw == HW - 1),
+            )
+
+        def new_accs():
+            return [
+                psum.tile([P, N], F32, tag="bank%d" % i, name="acc%d" % i) for i in range(SH * CH)
+            ]
+
+        def leave(osb, accs, half, s0, j):
+            for a in range(CH):
+                nc.scalar.copy(out=osb[:, j, a * N : (a + 1) * N], in_=accs[j * CH + a][:])
+            if j % 2 == 1:
+                nc.sync.dma_start(
+                    out=out_view[
+                        :, s0 + j - 1 : s0 + j + 1, half * CH * N : (half + 1) * CH * N
+                    ],
+                    in_=osb[:, j - 1 : j + 1, :],
+                )
+
+        for half in range(CT // CH):
+            accs = new_accs()
+            for hw in range(HW):
+                k = half * HW + hw
+                prepare_chunk(k)
+                if k + WBUFS < len(chunks):
+                    load_chunk(k + WBUFS)
+                for j in range(SH):
+                    for a in range(CH):
+                        mx_pass(accs[j * CH + a], j, half * CH + a, hw)
+            osb = big.tile([P, SH, CH * N], F32, tag="big", name="osb")
+            for j in range(SH):
+                leave(osb, accs, half, 0, j)
+            accs = new_accs()
+            osb = big.tile([P, SH, CH * N], F32, tag="big", name="osb")
+            for j in range(SH):
+                for a in range(CH):
+                    for hw in range(HW):
+                        mx_pass(accs[j * CH + a], SH + j, half * CH + a, hw)
+                leave(osb, accs, half, SH, j)

@@ -19,12 +19,13 @@ CT = 4
 CW = C // CT
 N = CW * 4
 TAPS = 9
-CH = 2
-SH = 4
-WBUFS = 4
+WBUFS = 5
+LEAD = 2
 
 FLOPS = 2 * B * (C * 4) * (O * HW)
 BYTES = 2 * (HW * O * C * 4) + 2 * (B * O * HW) + 4 * (B * C * 4)
+
+LOADS = [(0, 2, 0), (0, 2, 1), (0, 2, 2), (0, 2, 3), (2, 2, 0), (2, 2, 1), (2, 2, 2), (2, 1, 3), (3, 1, 3)]
 
 
 def tile_locallyconnected2d_t_kernel(tc, x, weights, grad_out, out):
@@ -32,7 +33,6 @@ def tile_locallyconnected2d_t_kernel(tc, x, weights, grad_out, out):
     g_view = grad_out.rearrange("(p s) o h w -> p s (o h w)", s=S)
     w_view = weights.rearrange("h w (t p) c i j -> (h w) p t (c i j)", p=P)
     out_view = out.rearrange("(p s) c r q -> p s (c r q)", s=S)
-    chunks = [(half, hw) for half in range(CT // CH) for hw in range(HW)]
 
     with ExitStack() as ctx:
         keep = ctx.enter_context(tc.tile_pool(name="keep", bufs=1))
@@ -62,15 +62,16 @@ def tile_locallyconnected2d_t_kernel(tc, x, weights, grad_out, out):
 
         w_raw = {}
 
-        def load_chunk(k):
-            half, hw = chunks[k]
-            wraw = wraw_pool.tile([P, T, CH * CW * TAPS], BF16, name="wraw")
-            width = CH * CW * TAPS
-            nc.sync.dma_start(out=wraw[:], in_=w_view[hw][:, :, half * width : (half + 1) * width])
+        def load_weights(k):
+            ct0, n_ct, hw = LOADS[k]
+            wraw = wraw_pool.tile([P, T, n_ct * CW * TAPS], BF16, tag="wraw", name="wraw")
+            nc.sync.dma_start(
+                out=wraw[:], in_=w_view[hw][:, :, ct0 * CW * TAPS : (ct0 + n_ct) * CW * TAPS]
+            )
             w_raw[k] = wraw
 
         for k in range(WBUFS):
-            load_chunk(k)
+            load_weights(k)
 
         def quantise_g(s, ggrp):
             nc.vector.quantize_mx(
@@ -98,25 +99,29 @@ def tile_locallyconnected2d_t_kernel(tc, x, weights, grad_out, out):
             waiting = ggrp
         quantise_g(S - 1, waiting)
 
-        def prepare_chunk(k):
-            half, hw = chunks[k]
+        def regroup(k, a, on_scalar=False):
+            hw = LOADS[k][2]
             h, w = hw // 2, hw % 2
             src = w_raw[k][:].rearrange("p t (c i j) -> p c t i j", i=3, j=3)
-            tiles = []
-            for a in range(CH):
-                wgrp = grp.tile([P, N * T], BF16, align_bytes=64, tag="grp", name="wgrp")
-                dst = wgrp[:].rearrange("p (c i j t) -> p c t i j", i=2, j=2, t=T)
-                for r in range(2):
-                    nc.vector.tensor_copy(
-                        out=dst[:, :, :, r, :],
-                        in_=src[:, a * CW : (a + 1) * CW, :, 1 - w + r, 1 - h : 3 - h],
-                    )
-                tiles.append(wgrp)
-            for a in range(CH):
-                idx = (half * CH + a) * HW + hw
-                nc.vector.quantize_mx(
-                    out=w_codes[:, idx, :].bitcast(E4X4), scales=w_scales[:, idx, :], in_=tiles[a][:]
-                )
+            wgrp = grp.tile([P, N * T], BF16, align_bytes=64, tag="grp", name="wgrp")
+            dst = wgrp[:].rearrange("p (c i j t) -> p c t i j", i=2, j=2, t=T)
+            for r in range(2):
+                taps = src[:, a * CW : (a + 1) * CW, :, 1 - w + r, 1 - h : 3 - h]
+                if on_scalar:
+                    nc.scalar.copy(out=dst[:, :, :, r, :], in_=taps)
+                else:
+                    nc.vector.tensor_copy(out=dst[:, :, :, r, :], in_=taps)
+            return wgrp
+
+        def quantise_w(k, a, wgrp):
+            idx = (LOADS[k][0] + a) * HW + LOADS[k][2]
+            nc.vector.quantize_mx(
+                out=w_codes[:, idx, :].bitcast(E4X4), scales=w_scales[:, idx, :], in_=wgrp[:]
+            )
+
+        def prepare(k):
+            for a in range(LOADS[k][1]):
+                quantise_w(k, a, regroup(k, a))
 
         def mx_pass(acc, s, ct, hw):
             idx = ct * HW + hw
@@ -131,38 +136,64 @@ def tile_locallyconnected2d_t_kernel(tc, x, weights, grad_out, out):
             )
 
         def new_accs():
-            return [
-                psum.tile([P, N], F32, tag="bank%d" % i, name="acc%d" % i) for i in range(SH * CH)
-            ]
+            return [psum.tile([P, N], F32, tag="bank%d" % s, name="acc%d" % s) for s in range(S)]
 
-        def leave(osb, accs, half, s0, j):
-            for a in range(CH):
-                nc.scalar.copy(out=osb[:, j, a * N : (a + 1) * N], in_=accs[j * CH + a][:])
-            if j % 2 == 1:
-                nc.sync.dma_start(
-                    out=out_view[
-                        :, s0 + j - 1 : s0 + j + 1, half * CH * N : (half + 1) * CH * N
-                    ],
-                    in_=osb[:, j - 1 : j + 1, :],
-                )
+        def new_rows():
+            return [big.tile([P, 4, 2 * N], F32, tag="big", name="osb") for quad in range(S // 4)]
 
-        for half in range(CT // CH):
-            accs = new_accs()
+        def leave(rows, accs, ct, s):
+            nc.scalar.copy(
+                out=rows[s // 4][:, s % 4, (ct % 2) * N : (ct % 2 + 1) * N], in_=accs[s][:]
+            )
+
+        def store(rows, half, s0, n_s):
+            nc.sync.dma_start(
+                out=out_view[:, s0 : s0 + n_s, half * 2 * N : (half + 1) * 2 * N],
+                in_=rows[s0 // 4][:, s0 % 4 : s0 % 4 + n_s, :],
+            )
+
+        accs = new_accs()
+        for hw in range(HW):
+            prepare(hw)
+            if hw + WBUFS < len(LOADS):
+                load_weights(hw + WBUFS)
+            for s in range(S):
+                mx_pass(accs[s], s, 0, hw)
+        rows = new_rows()
+        for s in range(S):
+            leave(rows, accs, 0, s)
+        accs = new_accs()
+        for s in range(S):
             for hw in range(HW):
-                k = half * HW + hw
-                prepare_chunk(k)
-                if k + WBUFS < len(chunks):
-                    load_chunk(k + WBUFS)
-                for j in range(SH):
-                    for a in range(CH):
-                        mx_pass(accs[j * CH + a], j, half * CH + a, hw)
-            osb = big.tile([P, SH, CH * N], F32, tag="big", name="osb")
-            for j in range(SH):
-                leave(osb, accs, half, 0, j)
-            accs = new_accs()
-            osb = big.tile([P, SH, CH * N], F32, tag="big", name="osb")
-            for j in range(SH):
-                for a in range(CH):
-                    for hw in range(HW):
-                        mx_pass(accs[j * CH + a], SH + j, half * CH + a, hw)
-                leave(osb, accs, half, SH, j)
+                mx_pass(accs[s], s, 1, hw)
+            leave(rows, accs, 1, s)
+            if s % 2 == 1:
+                store(rows, 0, s - 1, 2)
+
+        accs = new_accs()
+        for hw in range(2):
+            prepare(HW + hw)
+            for s in range(S):
+                mx_pass(accs[s], s, 2, hw)
+        quantise_w(6, 0, regroup(6, 0))
+        late = regroup(6, 1, on_scalar=True)
+        for s in range(S):
+            mx_pass(accs[s], s, 2, 2)
+        prepare(7)
+        for s in range(S):
+            mx_pass(accs[s], s, 2, 3)
+        quantise_w(6, 1, late)
+        prepare(8)
+        rows = new_rows()
+        for s in range(S):
+            leave(rows, accs, 2, s)
+        accs = new_accs()
+        for s in range(LEAD):
+            for hw in range(HW - 1):
+                mx_pass(accs[s], s, 3, hw)
+        for s in range(S):
+            for hw in range(HW):
+                if s >= LEAD or hw == HW - 1:
+                    mx_pass(accs[s], s, 3, hw)
+            leave(rows, accs, 3, s)
+            store(rows, 1, s, 1)

@@ -20,12 +20,11 @@ CW = C // CT
 N = CW * 4
 TAPS = 9
 WBUFS = 5
-LEAD = 2
 
 FLOPS = 2 * B * (C * 4) * (O * HW)
 BYTES = 2 * (HW * O * C * 4) + 2 * (B * O * HW) + 4 * (B * C * 4)
 
-LOADS = [(0, 2, 0), (0, 2, 1), (0, 2, 2), (0, 2, 3), (2, 2, 0), (2, 2, 1), (2, 2, 2), (2, 1, 3), (3, 1, 3)]
+LOADS = [(0, 2, 0), (0, 2, 1), (0, 2, 2), (0, 2, 3), (2, 2, 0), (2, 2, 1), (2, 2, 2), (2, 2, 3)]
 
 
 def tile_locallyconnected2d_t_kernel(tc, x, weights, grad_out, out):
@@ -99,7 +98,7 @@ def tile_locallyconnected2d_t_kernel(tc, x, weights, grad_out, out):
             waiting = ggrp
         quantise_g(S - 1, waiting)
 
-        def regroup(k, a, on_scalar=False):
+        def regroup(k, a):
             hw = LOADS[k][2]
             h, w = hw // 2, hw % 2
             src = w_raw[k][:].rearrange("p t (c i j) -> p c t i j", i=3, j=3)
@@ -107,10 +106,7 @@ def tile_locallyconnected2d_t_kernel(tc, x, weights, grad_out, out):
             dst = wgrp[:].rearrange("p (c i j t) -> p c t i j", i=2, j=2, t=T)
             for r in range(2):
                 taps = src[:, a * CW : (a + 1) * CW, :, 1 - w + r, 1 - h : 3 - h]
-                if on_scalar:
-                    nc.scalar.copy(out=dst[:, :, :, r, :], in_=taps)
-                else:
-                    nc.vector.tensor_copy(out=dst[:, :, :, r, :], in_=taps)
+                nc.vector.tensor_copy(out=dst[:, :, :, r, :], in_=taps)
             return wgrp
 
         def quantise_w(k, a, wgrp):
@@ -152,48 +148,23 @@ def tile_locallyconnected2d_t_kernel(tc, x, weights, grad_out, out):
                 in_=rows[s0 // 4][:, s0 % 4 : s0 % 4 + n_s, :],
             )
 
-        accs = new_accs()
-        for hw in range(HW):
-            prepare(hw)
-            if hw + WBUFS < len(LOADS):
-                load_weights(hw + WBUFS)
-            for s in range(S):
-                mx_pass(accs[s], s, 0, hw)
-        rows = new_rows()
-        for s in range(S):
-            leave(rows, accs, 0, s)
-        accs = new_accs()
-        for s in range(S):
+        for half in range(2):
+            accs = new_accs()
             for hw in range(HW):
-                mx_pass(accs[s], s, 1, hw)
-            leave(rows, accs, 1, s)
-            if s % 2 == 1:
-                store(rows, 0, s - 1, 2)
-
-        accs = new_accs()
-        for hw in range(2):
-            prepare(HW + hw)
+                k = half * HW + hw
+                prepare(k)
+                if k + WBUFS < len(LOADS):
+                    load_weights(k + WBUFS)
+                for s in range(S):
+                    mx_pass(accs[s], s, 2 * half, hw)
+            rows = new_rows()
             for s in range(S):
-                mx_pass(accs[s], s, 2, hw)
-        quantise_w(6, 0, regroup(6, 0))
-        late = regroup(6, 1, on_scalar=True)
-        for s in range(S):
-            mx_pass(accs[s], s, 2, 2)
-        prepare(7)
-        for s in range(S):
-            mx_pass(accs[s], s, 2, 3)
-        quantise_w(6, 1, late)
-        prepare(8)
-        rows = new_rows()
-        for s in range(S):
-            leave(rows, accs, 2, s)
-        accs = new_accs()
-        for s in range(LEAD):
-            for hw in range(HW - 1):
-                mx_pass(accs[s], s, 3, hw)
-        for s in range(S):
-            for hw in range(HW):
-                if s >= LEAD or hw == HW - 1:
-                    mx_pass(accs[s], s, 3, hw)
-            leave(rows, accs, 3, s)
-            store(rows, 1, s, 1)
+                leave(rows, accs, 2 * half, s)
+            accs = new_accs()
+            n_s = 2 - half
+            for s in range(S):
+                for hw in range(HW):
+                    mx_pass(accs[s], s, 2 * half + 1, hw)
+                leave(rows, accs, 2 * half + 1, s)
+                if s % n_s == n_s - 1:
+                    store(rows, half, s - n_s + 1, n_s)

@@ -19,25 +19,25 @@ CT = 4
 CW = C // CT
 N = CW * 4
 TAPS = 9
-WBUFS = 5
+WBUFS = 3
 
 FLOPS = 2 * B * (C * 4) * (O * HW)
 BYTES = 2 * (HW * O * C * 4) + 2 * (B * O * HW) + 4 * (B * C * 4)
 
-LOADS = [(0, 2, 0), (0, 2, 1), (0, 2, 2), (0, 2, 3), (2, 2, 0), (2, 2, 1), (2, 2, 2), (2, 2, 3)]
+LOADS = [(0, 4, 0), (0, 2, 1), (0, 2, 2), (0, 2, 3), (2, 2, 1), (2, 2, 2), (2, 2, 3)]
 
 
 def tile_locallyconnected2d_t_kernel(tc, x, weights, grad_out, out):
     nc = tc.nc
     g_view = grad_out.rearrange("(p s) o h w -> p s (o h w)", s=S)
-    w_view = weights.rearrange("h w (t p) c i j -> (h w) p t (c i j)", p=P)
+    w_view = weights.rearrange("h w (p t) c i j -> (h w) p t (c i j)", t=T)
     out_view = out.rearrange("(p s) c r q -> p s (c r q)", s=S)
 
     with ExitStack() as ctx:
         keep = ctx.enter_context(tc.tile_pool(name="keep", bufs=1))
         big = ctx.enter_context(tc.tile_pool(name="big", bufs=4))
         grp = ctx.enter_context(tc.tile_pool(name="grp", bufs=4))
-        wraw_pool = ctx.enter_context(tc.tile_pool(name="wraw", bufs=WBUFS))
+        wraw_pool = ctx.enter_context(tc.tile_pool(name="wraw", bufs=1))
         psum = ctx.enter_context(tc.psum_pool(name="psum", bufs=1))
         ctx.enter_context(tc.manual_schedule())
 
@@ -63,13 +63,15 @@ def tile_locallyconnected2d_t_kernel(tc, x, weights, grad_out, out):
 
         def load_weights(k):
             ct0, n_ct, hw = LOADS[k]
-            wraw = wraw_pool.tile([P, T, n_ct * CW * TAPS], BF16, tag="wraw", name="wraw")
+            tag = "whole" if n_ct == CT else "half"
+            bufs = 1 if n_ct == CT else WBUFS
+            wraw = wraw_pool.tile([P, T, n_ct * CW * TAPS], BF16, tag=tag, bufs=bufs, name="wraw")
             nc.sync.dma_start(
                 out=wraw[:], in_=w_view[hw][:, :, ct0 * CW * TAPS : (ct0 + n_ct) * CW * TAPS]
             )
             w_raw[k] = wraw
 
-        for k in range(WBUFS):
+        for k in range(1 + WBUFS):
             load_weights(k)
 
         def quantise_g(s, ggrp):
@@ -80,7 +82,7 @@ def tile_locallyconnected2d_t_kernel(tc, x, weights, grad_out, out):
         waiting = None
         for s in range(S):
             words = g_raw[s // 4][:, s % 4, :].bitcast(F32).rearrange(
-                "p (t o h) -> p t h o", t=T, o=P, h=2
+                "p (o t h) -> p t h o", t=T, o=P, h=2
             )
             ggrp = grp.tile([P, HW * P * T], BF16, align_bytes=64, tag="grp", name="ggrp")
             dst = ggrp[:].rearrange("p (a b t) -> p a b t", a=HW, b=P, t=T)
@@ -115,8 +117,8 @@ def tile_locallyconnected2d_t_kernel(tc, x, weights, grad_out, out):
                 out=w_codes[:, idx, :].bitcast(E4X4), scales=w_scales[:, idx, :], in_=wgrp[:]
             )
 
-        def prepare(k):
-            for a in range(LOADS[k][1]):
+        def prepare(k, a0):
+            for a in range(a0, a0 + 2):
                 quantise_w(k, a, regroup(k, a))
 
         def mx_pass(acc, s, ct, hw):
@@ -151,9 +153,9 @@ def tile_locallyconnected2d_t_kernel(tc, x, weights, grad_out, out):
         for half in range(2):
             accs = new_accs()
             for hw in range(HW):
-                k = half * HW + hw
-                prepare(k)
-                if k + WBUFS < len(LOADS):
+                k = hw if half == 0 or hw == 0 else HW - 1 + hw
+                prepare(k, 2 if half == 1 and hw == 0 else 0)
+                if 0 < k and k + WBUFS < len(LOADS):
                     load_weights(k + WBUFS)
                 for s in range(S):
                     mx_pass(accs[s], s, 2 * half, hw)

@@ -9,6 +9,7 @@ U32 = mybir.dt.uint32
 U8 = mybir.dt.uint8
 E4X4 = mybir.dt.float8_e4m3fn_x4
 E5X4 = mybir.dt.float8_e5m2_x4
+ADD = mybir.AluOpType.add
 
 P = 128
 B, C, O = 1024, 512, 512
@@ -19,12 +20,17 @@ CT = 4
 CW = C // CT
 N = CW * 4
 TAPS = 9
-WBUFS = 3
+W_SLOTS = 3
+WBUFS = 5
+HELD = 4
 
 FLOPS = 2 * B * (C * 4) * (O * HW)
 BYTES = 2 * (HW * O * C * 4) + 2 * (B * O * HW) + 4 * (B * C * 4)
 
-LOADS = [(0, 4, 0), (0, 2, 1), (0, 2, 2), (0, 2, 3), (2, 2, 1), (2, 2, 2), (2, 2, 3)]
+LOADS = [(2 * half, 2, hw) for half in range(2) for hw in range(HW)]
+WHERE = {
+    (ct0 + a, hw): k for k, (ct0, n_ct, hw) in enumerate(LOADS) for a in range(n_ct)
+}
 
 
 def tile_locallyconnected2d_t_kernel(tc, x, weights, grad_out, out):
@@ -37,7 +43,7 @@ def tile_locallyconnected2d_t_kernel(tc, x, weights, grad_out, out):
         keep = ctx.enter_context(tc.tile_pool(name="keep", bufs=1))
         big = ctx.enter_context(tc.tile_pool(name="big", bufs=4))
         grp = ctx.enter_context(tc.tile_pool(name="grp", bufs=4))
-        wraw_pool = ctx.enter_context(tc.tile_pool(name="wraw", bufs=1))
+        wraw_pool = ctx.enter_context(tc.tile_pool(name="wraw", bufs=WBUFS))
         psum = ctx.enter_context(tc.psum_pool(name="psum", bufs=1))
         ctx.enter_context(tc.manual_schedule())
 
@@ -46,8 +52,8 @@ def tile_locallyconnected2d_t_kernel(tc, x, weights, grad_out, out):
 
         g_codes = keep.tile([P, S, HW * P], U32, align_bytes=64)
         g_scales = keep.tile([P, S, HW * P], U8, align_bytes=64)
-        w_codes = keep.tile([P, CT * HW, N], U32, align_bytes=64)
-        w_scales = keep.tile([P, CT * HW, N], U8, align_bytes=64)
+        w_codes = keep.tile([P, W_SLOTS * HW, N], U32, align_bytes=64)
+        w_scales = keep.tile([P, W_SLOTS * HW, N], U8, align_bytes=64)
 
         g_raw = []
         for quad in range(S // 4):
@@ -63,15 +69,13 @@ def tile_locallyconnected2d_t_kernel(tc, x, weights, grad_out, out):
 
         def load_weights(k):
             ct0, n_ct, hw = LOADS[k]
-            tag = "whole" if n_ct == CT else "half"
-            bufs = 1 if n_ct == CT else WBUFS
-            wraw = wraw_pool.tile([P, T, n_ct * CW * TAPS], BF16, tag=tag, bufs=bufs, name="wraw")
+            wraw = wraw_pool.tile([P, T, n_ct * CW * TAPS], BF16, tag="wraw", name="wraw")
             nc.sync.dma_start(
                 out=wraw[:], in_=w_view[hw][:, :, ct0 * CW * TAPS : (ct0 + n_ct) * CW * TAPS]
             )
             w_raw[k] = wraw
 
-        for k in range(1 + WBUFS):
+        for k in range(WBUFS):
             load_weights(k)
 
         def quantise_g(s, ggrp):
@@ -91,58 +95,64 @@ def tile_locallyconnected2d_t_kernel(tc, x, weights, grad_out, out):
                 for t in range(T):
                     nc.tensor.transpose(xt[:, t * P : (t + 1) * P], words[:, t, h, :], ident[:])
                 src = xt[:].bitcast(BF16).rearrange("p (t b w) -> p w b t", t=T, b=P, w=2)
-                if h == 0:
+                if h == 0 and s % 4 != 2:
                     nc.vector.tensor_copy(out=dst[:, 0:2, :, :], in_=src)
                 else:
-                    nc.scalar.copy(out=dst[:, 2:4, :, :], in_=src)
+                    nc.scalar.copy(out=dst[:, 2 * h : 2 * h + 2, :, :], in_=src)
             if waiting is not None:
                 quantise_g(s - 1, waiting)
             waiting = ggrp
         quantise_g(S - 1, waiting)
 
-        def regroup(k, a):
-            hw = LOADS[k][2]
-            h, w = hw // 2, hw % 2
-            src = w_raw[k][:].rearrange("p t (c i j) -> p c t i j", i=3, j=3)
-            wgrp = grp.tile([P, N * T], BF16, align_bytes=64, tag="grp", name="wgrp")
-            dst = wgrp[:].rearrange("p (c i j t) -> p c t i j", i=2, j=2, t=T)
-            for r in range(2):
-                taps = src[:, a * CW : (a + 1) * CW, :, 1 - w + r, 1 - h : 3 - h]
-                nc.vector.tensor_copy(out=dst[:, :, :, r, :], in_=taps)
-            return wgrp
+        grouped = {}
 
-        def quantise_w(k, a, wgrp):
-            idx = (LOADS[k][0] + a) * HW + LOADS[k][2]
+        def regroup(copy, tag, ct, hw):
+            k = WHERE[(ct, hw)]
+            a = ct - LOADS[k][0]
+            h, w = hw // 2, hw % 2
+            src = w_raw[k][:].rearrange("p t (c i j) -> p c i t j", i=3, j=3)
+            wgrp = grp.tile([P, N * T], BF16, align_bytes=64, tag=tag, bufs=4 if tag == "grp" else 2, name="wgrp")
+            dst = wgrp[:].rearrange("p (c i j t) -> p c i t j", i=2, j=2, t=T)
+            copy(
+                out=dst,
+                in_=src[:, a * CW : (a + 1) * CW, 1 - w : 3 - w, :, 1 - h : 3 - h],
+            )
+            grouped[(ct, hw)] = wgrp
+
+        def vector_regroup(ct, hw):
+            regroup(nc.vector.tensor_copy, "grp", ct, hw)
+
+        def scalar_regroup(ct, hw):
+            regroup(nc.scalar.copy, "sgrp", ct, hw)
+
+        def slot(ct, hw):
+            return ct % W_SLOTS * HW + hw
+
+        def quantise_w(ct, hw):
+            idx = slot(ct, hw)
             nc.vector.quantize_mx(
-                out=w_codes[:, idx, :].bitcast(E4X4), scales=w_scales[:, idx, :], in_=wgrp[:]
+                out=w_codes[:, idx, :].bitcast(E4X4),
+                scales=w_scales[:, idx, :],
+                in_=grouped[(ct, hw)][:],
             )
 
-        def prepare(k, a0):
-            for a in range(a0, a0 + 2):
-                quantise_w(k, a, regroup(k, a))
-
-        def mx_pass(acc, s, ct, hw):
-            idx = ct * HW + hw
+        def mx_pass(acc, s, ct, hw, first, last):
+            idx = slot(ct, hw)
             nc.tensor.matmul_mx(
                 out=acc[:],
                 lhsT=g_codes[:, s, hw * P : (hw + 1) * P].bitcast(E5X4),
                 lhsT_scale=g_scales[:, s, hw * P : (hw + 1) * P],
                 rhs=w_codes[:, idx, :].bitcast(E4X4),
                 rhs_scale=w_scales[:, idx, :],
-                start=(hw == 0),
-                stop=(hw == HW - 1),
+                start=(hw == first),
+                stop=(hw == last),
             )
-
-        def new_accs():
-            return [psum.tile([P, N], F32, tag="bank%d" % s, name="acc%d" % s) for s in range(S)]
 
         def new_rows():
             return [big.tile([P, 4, 2 * N], F32, tag="big", name="osb") for quad in range(S // 4)]
 
-        def leave(rows, accs, ct, s):
-            nc.scalar.copy(
-                out=rows[s // 4][:, s % 4, (ct % 2) * N : (ct % 2 + 1) * N], in_=accs[s][:]
-            )
+        def place(rows, ct, s):
+            return rows[s // 4][:, s % 4, (ct % 2) * N : (ct % 2 + 1) * N]
 
         def store(rows, half, s0, n_s):
             nc.sync.dma_start(
@@ -150,23 +160,118 @@ def tile_locallyconnected2d_t_kernel(tc, x, weights, grad_out, out):
                 in_=rows[s0 // 4][:, s0 % 4 : s0 % 4 + n_s, :],
             )
 
-        for half in range(2):
-            accs = new_accs()
-            for hw in range(HW):
-                k = hw if half == 0 or hw == 0 else HW - 1 + hw
-                prepare(k, 2 if half == 1 and hw == 0 else 0)
-                if 0 < k and k + WBUFS < len(LOADS):
-                    load_weights(k + WBUFS)
-                for s in range(S):
-                    mx_pass(accs[s], s, 2 * half, hw)
-            rows = new_rows()
-            for s in range(S):
-                leave(rows, accs, 2 * half, s)
-            accs = new_accs()
-            n_s = 2 - half
-            for s in range(S):
-                for hw in range(HW):
-                    mx_pass(accs[s], s, 2 * half + 1, hw)
-                leave(rows, accs, 2 * half + 1, s)
-                if s % n_s == n_s - 1:
-                    store(rows, half, s - n_s + 1, n_s)
+        turn = [0]
+
+        def new_acc():
+            bank = HELD + turn[0] % (8 - HELD)
+            turn[0] += 1
+            return psum.tile([P, N], F32, tag="bank%d" % bank, name="acc")
+
+        def pair_sum(ct, s, hw0):
+            acc = new_acc()
+            for hw in (hw0, hw0 + 1):
+                mx_pass(acc, s, ct, hw, hw0, hw0 + 1)
+            return acc
+
+        def begin(ct):
+            accs = []
+            for s in range(HELD, S):
+                acc = new_acc()
+                mx_pass(acc, s, ct, 0, 0, 1)
+                accs.append(acc)
+            return accs
+
+        def end_spill(accs, rows, ct):
+            for s in range(HELD, S):
+                mx_pass(accs[s - HELD], s, ct, 1, 0, 1)
+                nc.scalar.copy(out=place(rows, ct, s), in_=accs[s - HELD][:])
+
+        def spill(rows, ct, s):
+            acc = pair_sum(ct, s, 0)
+            nc.scalar.copy(out=place(rows, ct, s), in_=acc[:])
+
+        def finish(rows, ct, s):
+            acc = pair_sum(ct, s, 2)
+            nc.vector.tensor_tensor(
+                out=place(rows, ct, s), in0=acc[:], in1=place(rows, ct, s), op=ADD
+            )
+
+        def hold(held, ct, hw):
+            for s in range(HELD):
+                mx_pass(held[s], s, ct, hw, 0, HW - 1)
+
+        def new_held():
+            return [psum.tile([P, N], F32, tag="bank%d" % s, name="held%d" % s) for s in range(HELD)]
+
+        held = new_held()
+        vector_regroup(0, 0)
+        scalar_regroup(1, 0)
+        quantise_w(0, 0)
+        hold(held, 0, 0)
+        begun = begin(0)
+        vector_regroup(0, 1)
+        quantise_w(1, 0)
+        load_weights(5)
+        scalar_regroup(1, 1)
+        quantise_w(0, 1)
+        quantise_w(1, 1)
+        load_weights(6)
+        hold(held, 0, 1)
+        rows = new_rows()
+        end_spill(begun, rows, 0)
+        for s in range(4):
+            spill(rows, 1, s)
+        for hw in (2, 3):
+            vector_regroup(0, hw)
+            quantise_w(0, hw)
+            vector_regroup(1, hw)
+            quantise_w(1, hw)
+            if hw == 2:
+                load_weights(7)
+            hold(held, 0, hw)
+            if hw == 2:
+                for s in range(4, S):
+                    spill(rows, 1, s)
+        for s in range(HELD):
+            nc.scalar.copy(out=place(rows, 0, s), in_=held[s][:])
+        scalar_regroup(2, 0)
+        scalar_regroup(3, 0)
+        for s in range(S):
+            if s >= HELD:
+                finish(rows, 0, s)
+            finish(rows, 1, s)
+            if s == 3:
+                quantise_w(2, 0)
+            if s == 6:
+                quantise_w(3, 0)
+            if s % 2 == 1:
+                store(rows, 0, s - 1, 2)
+
+        held = new_held()
+        hold(held, 2, 0)
+        begun = begin(2)
+        vector_regroup(2, 1)
+        scalar_regroup(3, 1)
+        quantise_w(2, 1)
+        quantise_w(3, 1)
+        hold(held, 2, 1)
+        rows = new_rows()
+        end_spill(begun, rows, 2)
+        for s in range(4):
+            spill(rows, 3, s)
+        for hw in (2, 3):
+            vector_regroup(2, hw)
+            quantise_w(2, hw)
+            vector_regroup(3, hw)
+            quantise_w(3, hw)
+            hold(held, 2, hw)
+            if hw == 2:
+                for s in range(4, S):
+                    spill(rows, 3, s)
+        for s in range(HELD):
+            nc.scalar.copy(out=place(rows, 2, s), in_=held[s][:])
+        for s in range(S):
+            if s >= HELD:
+                finish(rows, 2, s)
+            finish(rows, 3, s)
+            store(rows, 1, s, 1)

@@ -9,7 +9,6 @@ U32 = mybir.dt.uint32
 U8 = mybir.dt.uint8
 E4X4 = mybir.dt.float8_e4m3fn_x4
 E5X4 = mybir.dt.float8_e5m2_x4
-ADD = mybir.AluOpType.add
 
 P = 128
 B, C, O = 1024, 512, 512
@@ -22,7 +21,6 @@ N = CW * 4
 TAPS = 9
 W_SLOTS = 3
 WBUFS = 5
-HELD = 4
 
 FLOPS = 2 * B * (C * 4) * (O * HW)
 BYTES = 2 * (HW * O * C * 4) + 2 * (B * O * HW) + 4 * (B * C * 4)
@@ -160,118 +158,70 @@ def tile_locallyconnected2d_t_kernel(tc, x, weights, grad_out, out):
                 in_=rows[s0 // 4][:, s0 % 4 : s0 % 4 + n_s, :],
             )
 
-        turn = [0]
+        def new_accs():
+            return [psum.tile([P, N], F32, tag="bank%d" % s, name="acc%d" % s) for s in range(S)]
 
-        def new_acc():
-            bank = HELD + turn[0] % (8 - HELD)
-            turn[0] += 1
-            return psum.tile([P, N], F32, tag="bank%d" % bank, name="acc")
+        def place_pass(accs, ct, hw):
+            for s in range(S):
+                mx_pass(accs[s], s, ct, hw, 0, HW - 1)
 
-        def pair_sum(ct, s, hw0):
-            acc = new_acc()
-            for hw in (hw0, hw0 + 1):
-                mx_pass(acc, s, ct, hw, hw0, hw0 + 1)
-            return acc
+        def leave(copy, rows, accs, ct, s):
+            copy(out=place(rows, ct, s), in_=accs[s][:])
 
-        def begin(ct):
-            accs = []
-            for s in range(HELD, S):
-                acc = new_acc()
-                mx_pass(acc, s, ct, 0, 0, 1)
-                accs.append(acc)
-            return accs
+        def full_sum(accs, ct, s):
+            for hw in range(HW):
+                mx_pass(accs[s], s, ct, hw, 0, HW - 1)
 
-        def end_spill(accs, rows, ct):
-            for s in range(HELD, S):
-                mx_pass(accs[s - HELD], s, ct, 1, 0, 1)
-                nc.scalar.copy(out=place(rows, ct, s), in_=accs[s - HELD][:])
-
-        def spill(rows, ct, s):
-            acc = pair_sum(ct, s, 0)
-            nc.scalar.copy(out=place(rows, ct, s), in_=acc[:])
-
-        def finish(rows, ct, s):
-            acc = pair_sum(ct, s, 2)
-            nc.vector.tensor_tensor(
-                out=place(rows, ct, s), in0=acc[:], in1=place(rows, ct, s), op=ADD
-            )
-
-        def hold(held, ct, hw):
-            for s in range(HELD):
-                mx_pass(held[s], s, ct, hw, 0, HW - 1)
-
-        def new_held():
-            return [psum.tile([P, N], F32, tag="bank%d" % s, name="held%d" % s) for s in range(HELD)]
-
-        held = new_held()
+        accs = new_accs()
         vector_regroup(0, 0)
-        scalar_regroup(1, 0)
+        vector_regroup(1, 0)
         quantise_w(0, 0)
-        hold(held, 0, 0)
-        begun = begin(0)
-        vector_regroup(0, 1)
         quantise_w(1, 0)
         load_weights(5)
-        scalar_regroup(1, 1)
-        quantise_w(0, 1)
-        quantise_w(1, 1)
-        load_weights(6)
-        hold(held, 0, 1)
-        rows = new_rows()
-        end_spill(begun, rows, 0)
-        for s in range(4):
-            spill(rows, 1, s)
-        for hw in (2, 3):
+        place_pass(accs, 0, 0)
+        for hw in range(1, HW):
             vector_regroup(0, hw)
+            if hw > 1:
+                quantise_w(1, hw - 1)
+                load_weights(4 + hw)
+            scalar_regroup(1, hw)
             quantise_w(0, hw)
-            vector_regroup(1, hw)
-            quantise_w(1, hw)
-            if hw == 2:
-                load_weights(7)
-            hold(held, 0, hw)
-            if hw == 2:
-                for s in range(4, S):
-                    spill(rows, 1, s)
-        for s in range(HELD):
-            nc.scalar.copy(out=place(rows, 0, s), in_=held[s][:])
-        scalar_regroup(2, 0)
-        scalar_regroup(3, 0)
+            place_pass(accs, 0, hw)
+        rows = new_rows()
         for s in range(S):
-            if s >= HELD:
-                finish(rows, 0, s)
-            finish(rows, 1, s)
+            leave(nc.scalar.copy, rows, accs, 0, s)
+        vector_regroup(2, 0)
+        quantise_w(1, HW - 1)
+        vector_regroup(3, 0)
+        quantise_w(2, 0)
+        accs = new_accs()
+        for s in range(S):
+            full_sum(accs, 1, s)
+            leave(nc.scalar.copy, rows, accs, 1, s)
             if s == 3:
-                quantise_w(2, 0)
-            if s == 6:
-                quantise_w(3, 0)
+                scalar_regroup(3, 1)
             if s % 2 == 1:
                 store(rows, 0, s - 1, 2)
+        scalar_regroup(3, 2)
 
-        held = new_held()
-        hold(held, 2, 0)
-        begun = begin(2)
-        vector_regroup(2, 1)
-        scalar_regroup(3, 1)
-        quantise_w(2, 1)
-        quantise_w(3, 1)
-        hold(held, 2, 1)
-        rows = new_rows()
-        end_spill(begun, rows, 2)
-        for s in range(4):
-            spill(rows, 3, s)
-        for hw in (2, 3):
+        accs = new_accs()
+        place_pass(accs, 2, 0)
+        for hw in range(1, HW):
             vector_regroup(2, hw)
-            quantise_w(2, hw)
-            vector_regroup(3, hw)
-            quantise_w(3, hw)
-            hold(held, 2, hw)
-            if hw == 2:
-                for s in range(4, S):
-                    spill(rows, 3, s)
-        for s in range(HELD):
-            nc.scalar.copy(out=place(rows, 2, s), in_=held[s][:])
+            if hw < HW - 1:
+                quantise_w(3, hw - 1)
+                quantise_w(2, hw)
+            else:
+                scalar_regroup(3, hw)
+                quantise_w(2, hw)
+                quantise_w(3, hw - 1)
+                quantise_w(3, hw)
+            place_pass(accs, 2, hw)
+        rows = new_rows()
         for s in range(S):
-            if s >= HELD:
-                finish(rows, 2, s)
-            finish(rows, 3, s)
+            leave(nc.scalar.copy if s % 2 == 0 else nc.vector.tensor_copy, rows, accs, 2, s)
+        accs = new_accs()
+        for s in range(S):
+            full_sum(accs, 3, s)
+            leave(nc.scalar.copy if s % 2 == 0 else nc.vector.tensor_copy, rows, accs, 3, s)
             store(rows, 1, s, 1)

@@ -20,12 +20,12 @@ CW = C // CT
 N = CW * 4
 TAPS = 9
 W_SLOTS = 3
-WBUFS = 5
+WBUFS = 3
 
 FLOPS = 2 * B * (C * 4) * (O * HW)
 BYTES = 2 * (HW * O * C * 4) + 2 * (B * O * HW) + 4 * (B * C * 4)
 
-LOADS = [(2 * half, 2, hw) for half in range(2) for hw in range(HW)]
+LOADS = [(0, 4, 0)] + [(2 * half, 2, hw) for half in range(2) for hw in range(1, HW)]
 WHERE = {
     (ct0 + a, hw): k for k, (ct0, n_ct, hw) in enumerate(LOADS) for a in range(n_ct)
 }
@@ -41,7 +41,7 @@ def tile_locallyconnected2d_t_kernel(tc, x, weights, grad_out, out):
         keep = ctx.enter_context(tc.tile_pool(name="keep", bufs=1))
         big = ctx.enter_context(tc.tile_pool(name="big", bufs=4))
         grp = ctx.enter_context(tc.tile_pool(name="grp", bufs=4))
-        wraw_pool = ctx.enter_context(tc.tile_pool(name="wraw", bufs=WBUFS))
+        wraw_pool = ctx.enter_context(tc.tile_pool(name="wraw", bufs=1))
         psum = ctx.enter_context(tc.psum_pool(name="psum", bufs=1))
         ctx.enter_context(tc.manual_schedule())
 
@@ -67,13 +67,15 @@ def tile_locallyconnected2d_t_kernel(tc, x, weights, grad_out, out):
 
         def load_weights(k):
             ct0, n_ct, hw = LOADS[k]
-            wraw = wraw_pool.tile([P, T, n_ct * CW * TAPS], BF16, tag="wraw", name="wraw")
+            tag = "whole" if n_ct == CT else "half"
+            bufs = 1 if n_ct == CT else WBUFS
+            wraw = wraw_pool.tile([P, T, n_ct * CW * TAPS], BF16, tag=tag, bufs=bufs, name="wraw")
             nc.sync.dma_start(
                 out=wraw[:], in_=w_view[hw][:, :, ct0 * CW * TAPS : (ct0 + n_ct) * CW * TAPS]
             )
             w_raw[k] = wraw
 
-        for k in range(WBUFS):
+        for k in range(1 + WBUFS):
             load_weights(k)
 
         def quantise_g(s, ggrp):
@@ -109,7 +111,7 @@ def tile_locallyconnected2d_t_kernel(tc, x, weights, grad_out, out):
             a = ct - LOADS[k][0]
             h, w = hw // 2, hw % 2
             src = w_raw[k][:].rearrange("p t (c i j) -> p c i t j", i=3, j=3)
-            wgrp = grp.tile([P, N * T], BF16, align_bytes=64, tag=tag, bufs=4 if tag == "grp" else 2, name="wgrp")
+            wgrp = grp.tile([P, N * T], BF16, align_bytes=64, tag=tag, bufs=4 if tag == "grp" else 3, name="wgrp")
             dst = wgrp[:].rearrange("p (c i j t) -> p c i t j", i=2, j=2, t=T)
             copy(
                 out=dst,
@@ -175,25 +177,28 @@ def tile_locallyconnected2d_t_kernel(tc, x, weights, grad_out, out):
         accs = new_accs()
         vector_regroup(0, 0)
         vector_regroup(1, 0)
+        scalar_regroup(2, 0)
+        scalar_regroup(3, 0)
         quantise_w(0, 0)
         quantise_w(1, 0)
-        load_weights(5)
         place_pass(accs, 0, 0)
+        late = [(2, 0), (3, 0)]
         for hw in range(1, HW):
             vector_regroup(0, hw)
             if hw > 1:
-                quantise_w(1, hw - 1)
-                load_weights(4 + hw)
+                for tile in late:
+                    quantise_w(*tile)
+                load_weights(2 + hw)
+                late = []
             scalar_regroup(1, hw)
+            late.append((1, hw))
             quantise_w(0, hw)
             place_pass(accs, 0, hw)
         rows = new_rows()
         for s in range(S):
             leave(nc.scalar.copy, rows, accs, 0, s)
-        vector_regroup(2, 0)
         quantise_w(1, HW - 1)
-        vector_regroup(3, 0)
-        quantise_w(2, 0)
+        load_weights(6)
         accs = new_accs()
         for s in range(S):
             full_sum(accs, 1, s)
@@ -209,7 +214,8 @@ def tile_locallyconnected2d_t_kernel(tc, x, weights, grad_out, out):
         for hw in range(1, HW):
             vector_regroup(2, hw)
             if hw < HW - 1:
-                quantise_w(3, hw - 1)
+                if hw > 1:
+                    quantise_w(3, hw - 1)
                 quantise_w(2, hw)
             else:
                 scalar_regroup(3, hw)

@@ -20,6 +20,7 @@ CW = C // CT
 N = CW * 4
 TAPS = 9
 W_SLOTS = 3
+PAD = 64
 WBUFS = 3
 
 FLOPS = 2 * B * (C * 4) * (O * HW)
@@ -48,10 +49,14 @@ def tile_locallyconnected2d_t_kernel(tc, x, weights, grad_out, out):
         ident = keep.tile([P, P], F32)
         make_identity(nc, ident[:])
 
-        g_codes = keep.tile([P, S, HW * P], U32, align_bytes=64)
-        g_scales = keep.tile([P, S, HW * P], U8, align_bytes=64)
-        w_codes = keep.tile([P, W_SLOTS * HW, N], U32, align_bytes=64)
-        w_scales = keep.tile([P, W_SLOTS * HW, N], U8, align_bytes=64)
+        w_words = keep.tile([P, W_SLOTS * HW * N + PAD // 4], U32, align_bytes=64)
+        w_bytes = keep.tile([P, W_SLOTS * HW * N + PAD], U8, align_bytes=64)
+        g_words = keep.tile([P, S * HW * P + PAD // 4], U32, align_bytes=64)
+        g_bytes = keep.tile([P, S * HW * P], U8, align_bytes=64)
+        w_codes = w_words[:, 0 : W_SLOTS * HW * N].rearrange("p (k n) -> p k n", n=N)
+        w_scales = w_bytes[:, 0 : W_SLOTS * HW * N].rearrange("p (k n) -> p k n", n=N)
+        g_codes = g_words[:, 0 : S * HW * P].rearrange("p (s n) -> p s n", n=HW * P)
+        g_scales = g_bytes[:].rearrange("p (s n) -> p s n", n=HW * P)
 
         g_raw = []
         for quad in range(S // 4):

@@ -9,6 +9,7 @@ U32 = mybir.dt.uint32
 U8 = mybir.dt.uint8
 E4X4 = mybir.dt.float8_e4m3fn_x4
 E5X4 = mybir.dt.float8_e5m2_x4
+ADD = mybir.AluOpType.add
 
 P = 128
 B, C, O = 1024, 512, 512
@@ -61,10 +62,11 @@ def tile_locallyconnected2d_t_kernel(tc, x, weights, grad_out, out):
         g_raw = []
         for quad in range(S // 4):
             graw = big.tile([P, 4, O * HW], BF16, tag="big", name="graw")
-            for pair in range(2):
+            n_s = 2 if quad == 0 else 4
+            for s in range(0, 4, n_s):
                 nc.sync.dma_start(
-                    out=graw[:, 2 * pair : 2 * pair + 2, :],
-                    in_=g_view[:, 4 * quad + 2 * pair : 4 * quad + 2 * pair + 2, :],
+                    out=graw[:, s : s + n_s, :],
+                    in_=g_view[:, 4 * quad + s : 4 * quad + s + n_s, :],
                 )
             g_raw.append(graw)
 
@@ -179,55 +181,96 @@ def tile_locallyconnected2d_t_kernel(tc, x, weights, grad_out, out):
             for hw in range(HW):
                 mx_pass(accs[s], s, ct, hw, 0, HW - 1)
 
-        accs = new_accs()
+        def one_acc(bank):
+            return psum.tile([P, N], F32, tag="bank%d" % bank, name="acc%d" % bank)
+
+        def passes(acc, ct, s, places, first, last):
+            for hw in places:
+                mx_pass(acc, s, ct, hw, first, last)
+
+        def spill(rows, ct, s, acc):
+            nc.scalar.copy(out=place(rows, ct, s), in_=acc[:])
+
+        def add_rest(rows, ct, s, bank):
+            acc = one_acc(bank)
+            passes(acc, ct, s, (2, 3), 2, 3)
+            nc.vector.tensor_tensor(
+                out=place(rows, ct, s), in0=acc[:], in1=place(rows, ct, s), op=ADD
+            )
+
         vector_regroup(0, 0)
-        vector_regroup(1, 0)
         scalar_regroup(2, 0)
         scalar_regroup(3, 0)
         quantise_w(0, 0)
+        vector_regroup(1, 0)
         quantise_w(1, 0)
-        place_pass(accs, 0, 0)
-        late = [(2, 0), (3, 0)]
-        for hw in range(1, HW):
-            vector_regroup(0, hw)
-            if hw > 1:
-                for tile in late:
-                    quantise_w(*tile)
-                load_weights(2 + hw)
-                late = []
-            scalar_regroup(1, hw)
-            late.append((1, hw))
-            quantise_w(0, hw)
-            place_pass(accs, 0, hw)
+        accs = [one_acc(s) for s in range(S)]
+        for s in range(S):
+            passes(accs[s], 0, s, (0,), 0, 3 if s < 4 else 1)
+        vector_regroup(0, 1)
+        quantise_w(2, 0)
+        quantise_w(0, 1)
+        vector_regroup(1, 1)
+        quantise_w(3, 0)
+        quantise_w(1, 1)
+        load_weights(4)
         rows = new_rows()
-        for s in range(S):
-            leave(nc.scalar.copy, rows, accs, 0, s)
-        quantise_w(1, HW - 1)
+        for s in range(4):
+            passes(accs[s], 0, s, (1,), 0, 3)
+        for s in range(4, S):
+            passes(accs[s], 0, s, (1,), 0, 1)
+            spill(rows, 0, s, accs[s])
+        for s in range(4):
+            acc = one_acc(4 + s)
+            passes(acc, 1, s, (0, 1), 0, 1)
+            spill(rows, 1, s, acc)
+        late = [one_acc(s) for s in range(4, S)]
+        for s in range(4, S):
+            passes(late[s - 4], 1, s, (0, 1), 0, 3)
+        vector_regroup(0, 2)
+        quantise_w(0, 2)
+        vector_regroup(1, 2)
+        quantise_w(1, 2)
+        load_weights(5)
+        for s in range(4):
+            passes(accs[s], 0, s, (2,), 0, 3)
+        for s in range(4, S):
+            passes(late[s - 4], 1, s, (2,), 0, 3)
+        vector_regroup(0, 3)
+        scalar_regroup(1, 3)
+        quantise_w(0, 3)
+        quantise_w(1, 3)
         load_weights(6)
-        accs = new_accs()
-        for s in range(S):
-            full_sum(accs, 1, s)
-            leave(nc.scalar.copy, rows, accs, 1, s)
-            if s == 3:
-                scalar_regroup(3, 1)
-            if s % 2 == 1:
-                store(rows, 0, s - 1, 2)
-        scalar_regroup(3, 2)
+        for s in range(4):
+            passes(accs[s], 0, s, (3,), 0, 3)
+            spill(rows, 0, s, accs[s])
+        for s in range(4, S):
+            passes(late[s - 4], 1, s, (3,), 0, 3)
+            spill(rows, 1, s, late[s - 4])
+        for s in range(4, S):
+            add_rest(rows, 0, s, s - 4)
+        scalar_regroup(2, 1)
+        scalar_regroup(3, 1)
+        for s in range(4):
+            add_rest(rows, 1, s, 4 + s)
+        quantise_w(2, 1)
+        for s in range(0, S, 2):
+            store(rows, 0, s, 2)
 
-        accs = new_accs()
+        accs = [one_acc(s) for s in range(S)]
         place_pass(accs, 2, 0)
-        for hw in range(1, HW):
-            vector_regroup(2, hw)
-            if hw < HW - 1:
-                if hw > 1:
-                    quantise_w(3, hw - 1)
-                quantise_w(2, hw)
-            else:
-                scalar_regroup(3, hw)
-                quantise_w(2, hw)
-                quantise_w(3, hw - 1)
-                quantise_w(3, hw)
-            place_pass(accs, 2, hw)
+        place_pass(accs, 2, 1)
+        scalar_regroup(3, 2)
+        vector_regroup(2, 2)
+        quantise_w(3, 1)
+        quantise_w(2, 2)
+        place_pass(accs, 2, 2)
+        vector_regroup(2, 3)
+        quantise_w(2, 3)
+        quantise_w(3, 2)
+        vector_regroup(3, 3)
+        quantise_w(3, 3)
+        place_pass(accs, 2, 3)
         rows = new_rows()
         for s in range(S):
             leave(nc.scalar.copy if s % 2 == 0 else nc.vector.tensor_copy, rows, accs, 2, s)

@@ -24,6 +24,8 @@ W_SLOTS = 3
 PAD = 64
 WBUFS = 3
 
+EARLY = (1, 3, 5, 7)
+
 FLOPS = 2 * B * (C * 4) * (O * HW)
 BYTES = 2 * (HW * O * C * 4) + 2 * (B * O * HW) + 4 * (B * C * 4)
 
@@ -50,12 +52,14 @@ def tile_locallyconnected2d_t_kernel(tc, x, weights, grad_out, out):
         ident = keep.tile([P, P], F32)
         make_identity(nc, ident[:])
 
-        w_words = keep.tile([P, W_SLOTS * HW * N + PAD // 4], U32, align_bytes=64)
-        w_bytes = keep.tile([P, W_SLOTS * HW * N + PAD], U8, align_bytes=64)
+        w_words = keep.tile([P, (W_SLOTS * HW + 1) * N + PAD // 4], U32, align_bytes=64)
+        w_bytes = keep.tile([P, (W_SLOTS * HW + 1) * (N + 2 * PAD) + 3 * PAD], U8, align_bytes=64)
         g_words = keep.tile([P, S * HW * P + PAD // 4], U32, align_bytes=64)
         g_bytes = keep.tile([P, S * HW * P], U8, align_bytes=64)
-        w_codes = w_words[:, 0 : W_SLOTS * HW * N].rearrange("p (k n) -> p k n", n=N)
-        w_scales = w_bytes[:, 0 : W_SLOTS * HW * N].rearrange("p (k n) -> p k n", n=N)
+        w_codes = w_words[:, 0 : (W_SLOTS * HW + 1) * N].rearrange("p (k n) -> p k n", n=N)
+        w_scales = w_bytes[:, 0 : (W_SLOTS * HW + 1) * (N + 2 * PAD)].rearrange(
+            "p (k n) -> p k n", n=N + 2 * PAD
+        )
         g_codes = g_words[:, 0 : S * HW * P].rearrange("p (s n) -> p s n", n=HW * P)
         g_scales = g_bytes[:].rearrange("p (s n) -> p s n", n=HW * P)
 
@@ -133,13 +137,13 @@ def tile_locallyconnected2d_t_kernel(tc, x, weights, grad_out, out):
             regroup(nc.scalar.copy, "sgrp", ct, hw)
 
         def slot(ct, hw):
-            return ct % W_SLOTS * HW + hw
+            return W_SLOTS * HW if (ct, hw) == (3, 0) else ct % W_SLOTS * HW + hw
 
         def quantise_w(ct, hw):
             idx = slot(ct, hw)
             nc.vector.quantize_mx(
                 out=w_codes[:, idx, :].bitcast(E4X4),
-                scales=w_scales[:, idx, :],
+                scales=w_scales[:, idx, 0:N],
                 in_=grouped[(ct, hw)][:],
             )
 
@@ -150,7 +154,7 @@ def tile_locallyconnected2d_t_kernel(tc, x, weights, grad_out, out):
                 lhsT=g_codes[:, s, hw * P : (hw + 1) * P].bitcast(E5X4),
                 lhsT_scale=g_scales[:, s, hw * P : (hw + 1) * P],
                 rhs=w_codes[:, idx, :].bitcast(E4X4),
-                rhs_scale=w_scales[:, idx, :],
+                rhs_scale=w_scales[:, idx, 0:N],
                 start=(hw == first),
                 stop=(hw == last),
             )
@@ -198,23 +202,31 @@ def tile_locallyconnected2d_t_kernel(tc, x, weights, grad_out, out):
                 out=place(rows, ct, s), in0=acc[:], in1=place(rows, ct, s), op=ADD
             )
 
+        rows = new_rows()
+        rows_b = new_rows()
         vector_regroup(0, 0)
-        scalar_regroup(2, 0)
         scalar_regroup(3, 0)
+        scalar_regroup(2, 0)
         quantise_w(0, 0)
         vector_regroup(1, 0)
+        quantise_w(3, 0)
         quantise_w(1, 0)
-        accs = [one_acc(s) for s in range(S)]
-        for s in range(S):
-            passes(accs[s], 0, s, (0,), 0, 3 if s < 4 else 1)
+        accs = [one_acc(s) for s in range(4)]
+        for s in range(4):
+            passes(accs[s], 0, s, (0,), 0, 3)
+        for s in EARLY:
+            acc = one_acc(4 + s // 2)
+            passes(acc, 3, s, (0,), 0, 0)
+            spill(rows_b, 3, s, acc)
+        accs += [one_acc(s) for s in range(4, S)]
+        for s in range(4, S):
+            passes(accs[s], 0, s, (0,), 0, 1)
         vector_regroup(0, 1)
         quantise_w(2, 0)
         quantise_w(0, 1)
         vector_regroup(1, 1)
-        quantise_w(3, 0)
         quantise_w(1, 1)
         load_weights(4)
-        rows = new_rows()
         for s in range(4):
             passes(accs[s], 0, s, (1,), 0, 3)
         for s in range(4, S):
@@ -271,11 +283,16 @@ def tile_locallyconnected2d_t_kernel(tc, x, weights, grad_out, out):
         vector_regroup(3, 3)
         quantise_w(3, 3)
         place_pass(accs, 2, 3)
-        rows = new_rows()
         for s in range(S):
-            leave(nc.scalar.copy if s % 2 == 0 else nc.vector.tensor_copy, rows, accs, 2, s)
-        accs = new_accs()
+            leave(nc.scalar.copy if s % 2 == 0 else nc.vector.tensor_copy, rows_b, accs, 2, s)
         for s in range(S):
-            full_sum(accs, 3, s)
-            leave(nc.scalar.copy if s % 2 == 0 else nc.vector.tensor_copy, rows, accs, 3, s)
-            store(rows, 1, s, 1)
+            acc = one_acc(s)
+            if s in EARLY:
+                passes(acc, 3, s, (1, 2, 3), 1, 3)
+                nc.vector.tensor_tensor(
+                    out=place(rows_b, 3, s), in0=acc[:], in1=place(rows_b, 3, s), op=ADD
+                )
+            else:
+                passes(acc, 3, s, (0, 1, 2, 3), 0, 3)
+                spill(rows_b, 3, s, acc)
+            store(rows_b, 1, s, 1)

from contextlib import ExitStack

import concourse.mybir as mybir
from concourse.masks import make_identity

F32 = mybir.dt.float32
BF16 = mybir.dt.bfloat16
U32 = mybir.dt.uint32
U8 = mybir.dt.uint8
E4X4 = mybir.dt.float8_e4m3fn_x4
E5X4 = mybir.dt.float8_e5m2_x4
ADD = mybir.AluOpType.add

P = 128
B, C, O = 1024, 512, 512
S = B // P
HW = 4
T = 4
CT = 4
CW = C // CT
N = CW * 4
TAPS = 9
W_SLOTS = 3
PAD = 64
WBUFS = 3

EARLY = (1, 3, 5, 7)

FLOPS = 2 * B * (C * 4) * (O * HW)
BYTES = 2 * (HW * O * C * 4) + 2 * (B * O * HW) + 4 * (B * C * 4)

LOADS = [(0, 4, 0)] + [(2 * half, 2, hw) for half in range(2) for hw in range(1, HW)]
WHERE = {
    (ct0 + a, hw): k for k, (ct0, n_ct, hw) in enumerate(LOADS) for a in range(n_ct)
}


def tile_locallyconnected2d_t_kernel(tc, x, weights, grad_out, out):
    nc = tc.nc
    g_view = grad_out.rearrange("(p s) o h w -> p s (o h w)", s=S)
    w_view = weights.rearrange("h w (p t) c i j -> (h w) p t (c i j)", t=T)
    out_view = out.rearrange("(p s) c r q -> p s (c r q)", s=S)

    with ExitStack() as ctx:
        keep = ctx.enter_context(tc.tile_pool(name="keep", bufs=1))
        big = ctx.enter_context(tc.tile_pool(name="big", bufs=4))
        grp = ctx.enter_context(tc.tile_pool(name="grp", bufs=4))
        wraw_pool = ctx.enter_context(tc.tile_pool(name="wraw", bufs=1))
        psum = ctx.enter_context(tc.psum_pool(name="psum", bufs=1))
        ctx.enter_context(tc.manual_schedule())

        ident = keep.tile([P, P], F32)
        make_identity(nc, ident[:])

        w_words = keep.tile([P, (W_SLOTS * HW + 1) * N + PAD // 4], U32, align_bytes=64)
        w_bytes = keep.tile([P, (W_SLOTS * HW + 1) * (N + 2 * PAD) + 3 * PAD], U8, align_bytes=64)
        g_words = keep.tile([P, S * HW * P + PAD // 4], U32, align_bytes=64)
        g_bytes = keep.tile([P, S * HW * P], U8, align_bytes=64)
        w_codes = w_words[:, 0 : (W_SLOTS * HW + 1) * N].rearrange("p (k n) -> p k n", n=N)
        w_scales = w_bytes[:, 0 : (W_SLOTS * HW + 1) * (N + 2 * PAD)].rearrange(
            "p (k n) -> p k n", n=N + 2 * PAD
        )
        g_codes = g_words[:, 0 : S * HW * P].rearrange("p (s n) -> p s n", n=HW * P)
        g_scales = g_bytes[:].rearrange("p (s n) -> p s n", n=HW * P)

        g_raw = []
        for quad in range(S // 4):
            graw = big.tile([P, 4, O * HW], BF16, tag="big", name="graw")
            n_s = 2 if quad == 0 else 4
            for s in range(0, 4, n_s):
                nc.sync.dma_start(
                    out=graw[:, s : s + n_s, :],
                    in_=g_view[:, 4 * quad + s : 4 * quad + s + n_s, :],
                )
            g_raw.append(graw)

        w_raw = {}

        def load_weights(k):
            ct0, n_ct, hw = LOADS[k]
            tag = "whole" if n_ct == CT else "half"
            bufs = 1 if n_ct == CT else WBUFS
            wraw = wraw_pool.tile([P, T, n_ct * CW * TAPS], BF16, tag=tag, bufs=bufs, name="wraw")
            nc.sync.dma_start(
                out=wraw[:], in_=w_view[hw][:, :, ct0 * CW * TAPS : (ct0 + n_ct) * CW * TAPS]
            )
            w_raw[k] = wraw

        for k in range(1 + WBUFS):
            load_weights(k)

        def quantise_g(s, ggrp):
            nc.vector.quantize_mx(
                out=g_codes[:, s, :].bitcast(E5X4), scales=g_scales[:, s, :], in_=ggrp[:]
            )

        waiting = None
        for s in range(S):
            words = g_raw[s // 4][:, s % 4, :].bitcast(F32).rearrange(
                "p (o t h) -> p t h o", t=T, o=P, h=2
            )
            ggrp = grp.tile([P, HW * P * T], BF16, align_bytes=64, tag="grp", name="ggrp")
            dst = ggrp[:].rearrange("p (a b t) -> p a b t", a=HW, b=P, t=T)
            for h in range(2):
                xt = psum.tile([P, T * P], F32, tag="bank%d" % ((2 * s + h) % 8), name="xt")
                for t in range(T):
                    nc.tensor.transpose(xt[:, t * P : (t + 1) * P], words[:, t, h, :], ident[:])
                src = xt[:].bitcast(BF16).rearrange("p (t b w) -> p w b t", t=T, b=P, w=2)
                if h == 0 and s % 4 != 2:
                    nc.vector.tensor_copy(out=dst[:, 0:2, :, :], in_=src)
                else:
                    nc.scalar.copy(out=dst[:, 2 * h : 2 * h + 2, :, :], in_=src)
            if waiting is not None:
                quantise_g(s - 1, waiting)
            waiting = ggrp
        quantise_g(S - 1, waiting)

        grouped = {}

        def regroup(copy, tag, ct, hw):
            k = WHERE[(ct, hw)]
            a = ct - LOADS[k][0]
            h, w = hw // 2, hw % 2
            src = w_raw[k][:].rearrange("p t (c i j) -> p c i t j", i=3, j=3)
            wgrp = grp.tile([P, N * T], BF16, align_bytes=64, tag=tag, bufs=4 if tag == "grp" else 3, name="wgrp")
            dst = wgrp[:].rearrange("p (c i j t) -> p c i t j", i=2, j=2, t=T)
            copy(
                out=dst,
                in_=src[:, a * CW : (a + 1) * CW, 1 - w : 3 - w, :, 1 - h : 3 - h],
            )
            grouped[(ct, hw)] = wgrp

        def vector_regroup(ct, hw):
            regroup(nc.vector.tensor_copy, "grp", ct, hw)

        def scalar_regroup(ct, hw):
            regroup(nc.scalar.copy, "sgrp", ct, hw)

        def slot(ct, hw):
            return W_SLOTS * HW if (ct, hw) == (3, 0) else ct % W_SLOTS * HW + hw

        def quantise_w(ct, hw):
            idx = slot(ct, hw)
            nc.vector.quantize_mx(
                out=w_codes[:, idx, :].bitcast(E4X4),
                scales=w_scales[:, idx, 0:N],
                in_=grouped[(ct, hw)][:],
            )

        def mx_pass(acc, s, ct, hw, first, last):
            idx = slot(ct, hw)
            nc.tensor.matmul_mx(
                out=acc[:],
                lhsT=g_codes[:, s, hw * P : (hw + 1) * P].bitcast(E5X4),
                lhsT_scale=g_scales[:, s, hw * P : (hw + 1) * P],
                rhs=w_codes[:, idx, :].bitcast(E4X4),
                rhs_scale=w_scales[:, idx, 0:N],
                start=(hw == first),
                stop=(hw == last),
            )

        def new_rows():
            return [big.tile([P, 4, 2 * N], F32, tag="big", name="osb") for quad in range(S // 4)]

        def place(rows, ct, s):
            return rows[s // 4][:, s % 4, (ct % 2) * N : (ct % 2 + 1) * N]

        def store(rows, half, s0, n_s):
            nc.sync.dma_start(
                out=out_view[:, s0 : s0 + n_s, half * 2 * N : (half + 1) * 2 * N],
                in_=rows[s0 // 4][:, s0 % 4 : s0 % 4 + n_s, :],
            )

        def new_accs():
            return [psum.tile([P, N], F32, tag="bank%d" % s, name="acc%d" % s) for s in range(S)]

        def place_pass(accs, ct, hw):
            for s in range(S):
                mx_pass(accs[s], s, ct, hw, 0, HW - 1)

        def leave(copy, rows, accs, ct, s):
            copy(out=place(rows, ct, s), in_=accs[s][:])

        def full_sum(accs, ct, s):
            for hw in range(HW):
                mx_pass(accs[s], s, ct, hw, 0, HW - 1)

        def one_acc(bank):
            return psum.tile([P, N], F32, tag="bank%d" % bank, name="acc%d" % bank)

        def passes(acc, ct, s, places, first, last):
            for hw in places:
                mx_pass(acc, s, ct, hw, first, last)

        def spill(rows, ct, s, acc):
            nc.scalar.copy(out=place(rows, ct, s), in_=acc[:])

        def add_rest(rows, ct, s, bank):
            acc = one_acc(bank)
            passes(acc, ct, s, (2, 3), 2, 3)
            nc.vector.tensor_tensor(
                out=place(rows, ct, s), in0=acc[:], in1=place(rows, ct, s), op=ADD
            )

        rows = new_rows()
        rows_b = new_rows()
        vector_regroup(0, 0)
        scalar_regroup(3, 0)
        scalar_regroup(2, 0)
        quantise_w(0, 0)
        vector_regroup(1, 0)
        quantise_w(3, 0)
        quantise_w(1, 0)
        accs = [one_acc(s) for s in range(4)]
        for s in range(4):
            passes(accs[s], 0, s, (0,), 0, 3)
        for s in EARLY:
            acc = one_acc(4 + s // 2)
            passes(acc, 3, s, (0,), 0, 0)
            spill(rows_b, 3, s, acc)
        accs += [one_acc(s) for s in range(4, S)]
        for s in range(4, S):
            passes(accs[s], 0, s, (0,), 0, 1)
        vector_regroup(0, 1)
        quantise_w(2, 0)
        quantise_w(0, 1)
        vector_regroup(1, 1)
        quantise_w(1, 1)
        load_weights(4)
        for s in range(4):
            passes(accs[s], 0, s, (1,), 0, 3)
        for s in range(4, S):
            passes(accs[s], 0, s, (1,), 0, 1)
            spill(rows, 0, s, accs[s])
        for s in range(4):
            acc = one_acc(4 + s)
            passes(acc, 1, s, (0, 1), 0, 1)
            spill(rows, 1, s, acc)
        late = [one_acc(s) for s in range(4, S)]
        for s in range(4, S):
            passes(late[s - 4], 1, s, (0, 1), 0, 3)
        vector_regroup(0, 2)
        quantise_w(0, 2)
        vector_regroup(1, 2)
        quantise_w(1, 2)
        load_weights(5)
        for s in range(4):
            passes(accs[s], 0, s, (2,), 0, 3)
        for s in range(4, S):
            passes(late[s - 4], 1, s, (2,), 0, 3)
        vector_regroup(0, 3)
        scalar_regroup(1, 3)
        quantise_w(0, 3)
        quantise_w(1, 3)
        load_weights(6)
        for s in range(4):
            passes(accs[s], 0, s, (3,), 0, 3)
            spill(rows, 0, s, accs[s])
        for s in range(4, S):
            passes(late[s - 4], 1, s, (3,), 0, 3)
            spill(rows, 1, s, late[s - 4])
        for s in range(4, S):
            add_rest(rows, 0, s, s - 4)
        scalar_regroup(2, 1)
        scalar_regroup(3, 1)
        for s in range(4):
            add_rest(rows, 1, s, 4 + s)
        quantise_w(2, 1)
        for s in range(0, S, 2):
            store(rows, 0, s, 2)

        accs = [one_acc(s) for s in range(S)]
        place_pass(accs, 2, 0)
        place_pass(accs, 2, 1)
        scalar_regroup(3, 2)
        vector_regroup(2, 2)
        quantise_w(3, 1)
        quantise_w(2, 2)
        place_pass(accs, 2, 2)
        vector_regroup(2, 3)
        quantise_w(2, 3)
        quantise_w(3, 2)
        vector_regroup(3, 3)
        quantise_w(3, 3)
        place_pass(accs, 2, 3)
        for s in range(S):
            leave(nc.scalar.copy if s % 2 == 0 else nc.vector.tensor_copy, rows_b, accs, 2, s)
        for s in range(S):
            acc = one_acc(s)
            if s in EARLY:
                passes(acc, 3, s, (1, 2, 3), 1, 3)
                nc.vector.tensor_tensor(
                    out=place(rows_b, 3, s), in0=acc[:], in1=place(rows_b, 3, s), op=ADD
                )
            else:
                passes(acc, 3, s, (0, 1, 2, 3), 0, 3)
                spill(rows_b, 3, s, acc)
            store(rows_b, 1, s, 1)
